import numpy as np
import ml_dtypes


def mxq(x, axis, fmt="e4m3"):
    dtype, down = {"e4m3": (ml_dtypes.float8_e4m3fn, 7), "e5m2": (ml_dtypes.float8_e5m2, 14)}[fmt]
    v = np.moveaxis(np.asarray(x, np.float32).astype(ml_dtypes.bfloat16).astype(np.float64), axis, -1)
    blocks = v.reshape(v.shape[:-1] + (-1, 32))
    amax = np.abs(blocks).max(-1, keepdims=True)
    byte = np.maximum(np.where(amax > 0, np.frexp(amax)[1] - 1 + 127, 0) - down, 1)
    scale = np.exp2(byte - 127.0)
    codes = (blocks / scale).astype(np.float32).astype(dtype).astype(np.float64)
    return np.moveaxis((codes * scale).reshape(v.shape), -1, axis)


WIDE = False


def mx_kscale(k):
    if not WIDE:
        return np.ones(k)
    levels = np.array([10, -10, 5, -5, 0])
    if k % 512:
        return np.exp2(np.random.permutation(np.resize(levels, k // 32))).repeat(32)
    a = np.empty((k // 512, 16))
    for p in range(k // 512):
        a[p, :8] = np.random.permutation(np.resize(levels, 8))
        for g in range(8):
            far = levels[np.abs(levels - a[p, g]) >= 10]
            a[p, g + 8] = far[np.random.randint(len(far))]
    return np.exp2(a.ravel()).repeat(32)


BF16 = ml_dtypes.bfloat16


def bf(x):
    return np.asarray(x, np.float32).astype(BF16)


def f64(x):
    return np.asarray(x).astype(np.float64)


B, CIN, R, COUT, H, W, D, KS = 2, 512, 512, 256, 16, 16, 16, 3
P = H * W * D
PAD = (KS - 1) // 2


def slice_in_dim(t, a, b, axis):
    idx = [slice(None)] * t.ndim
    idx[axis] = slice(a, b)
    return t[tuple(idx)]


def axis_contract(t, U, axis):
    L = t.shape[axis] - (KS - 1)
    rshape = (1, U.shape[1], 1, 1, 1)
    acc = slice_in_dim(t, 0, L, axis) * U[0].reshape(rshape)
    for k in range(1, KS):
        acc = acc + slice_in_dim(t, k, k + L, axis) * U[k].reshape(rshape)
    return acc


def draw0():
    s, t = mx_kscale(CIN), mx_kscale(R)
    return {"x": bf(np.random.standard_normal((B, CIN, H, W, D)) * s[None, :, None, None, None]),
            "U_kh": bf(np.random.standard_normal((KS, R)) / np.sqrt(KS)),
            "U_kw": bf(np.random.standard_normal((KS, R)) / np.sqrt(KS)),
            "U_kd": bf(np.random.standard_normal((KS, R)) / np.sqrt(KS)),
            "U_c_in": bf(np.random.standard_normal((CIN, R)) / np.sqrt(CIN) / s[:, None] * t[None, :]),
            "U_c_out": bf(np.random.standard_normal((R, COUT)) / np.sqrt(R) / t[:, None]),
            "bias": bf(np.random.standard_normal(COUT) * 0.5)}


def core(x, U_kh, U_kw, U_kd, U_c_in, U_c_out, bias):
    xq = mxq(f64(x), 1, "e4m3").reshape(B, CIN, P)
    y = (mxq(f64(U_c_in), 0, "e4m3").T @ xq).reshape(B, R, H, W, D)
    y = np.pad(y, ((0, 0), (0, 0), (PAD, PAD), (PAD, PAD), (PAD, PAD)))
    y = axis_contract(y, f64(U_kh), 2)
    y = axis_contract(y, f64(U_kw), 3)
    y = axis_contract(y, f64(U_kd), 4)
    out = (mxq(f64(U_c_out), 0, "e4m3").T @ mxq(y, 1, "e4m3").reshape(B, R, P)).reshape(B, COUT, H, W, D)
    return out + f64(bias)[None, :, None, None, None]


def e4m3fn_bytes(y):
    return np.clip(np.asarray(y, np.float64), -448.0, 448.0).astype(np.float32).astype(ml_dtypes.float8_e4m3fn).view(np.uint8)


def e4m3fn_values(b):
    return np.asarray(b, np.uint8).view(ml_dtypes.float8_e4m3fn).astype(np.float64)


def setup_inputs():
    d = draw0()
    x0 = np.asarray(d['x']).astype(np.float64)
    s = (np.max(np.abs(x0), axis=(0, 2, 3, 4), keepdims=True) / 448.0).astype(np.float32)
    out = {}
    for k, v in d.items():
        if k == 'x':
            out['x_bytes'] = e4m3fn_bytes(x0 / s.astype(np.float64))
            out['x_scale'] = s
        else:
            out[k] = v
    return out


def reference(x_bytes, x_scale, U_kh, U_kw, U_kd, U_c_in, U_c_out, bias):
    return core(e4m3fn_values(x_bytes) * x_scale.astype(np.float64), U_kh, U_kw, U_kd, U_c_in, U_c_out, bias)

@@ -1,0 +1,394 @@
+from contextlib import ExitStack
+
+import concourse.mybir as mybir
+from concourse.masks import make_identity
+
+F32 = mybir.dt.float32
+BF16 = mybir.dt.bfloat16
+U32 = mybir.dt.uint32
+U8 = mybir.dt.uint8
+FP8 = mybir.dt.float8_e4m3fn
+FP8X4 = mybir.dt.float8_e4m3fn_x4
+ADD = mybir.AluOpType.add
+SUB = mybir.AluOpType.subtract
+MULT = mybir.AluOpType.mult
+MAX = mybir.AluOpType.max
+LT = mybir.AluOpType.is_lt
+COPY = mybir.ActivationFunctionType.Copy
+IDENT = mybir.ActivationFunctionType.Identity
+
+P = 128
+T = 4
+BATCH, CIN, RANK, COUT, SIDE = 2, 512, 512, 256, 16
+PLANE = SIDE * SIDE
+VOL = SIDE * PLANE
+COLS = 512
+STEPS = BATCH * VOL // COLS
+STEPS_B = VOL // COLS
+PITCH = 20
+RING = 8
+PE_ROWS = 6
+CX_S = 384
+
+FLOPS = 2 * BATCH * VOL * RANK * (CIN + COUT)
+
+
+def tile_lowrankconv3d_t_kernel(tc, x_bytes, x_scale, U_kh, U_kw, U_kd, U_c_in, U_c_out, bias, out):
+    nc = tc.nc
+    units = []
+    for s in range(STEPS + 1):
+        b, j = divmod(s, STEPS_B)
+        segs = []
+        if j == 0:
+            if s > 0:
+                segs.append((b - 1, SIDE - 1, 1))
+            if s < STEPS:
+                segs.append((b, 0, 1))
+        elif (2 * j) % RING == 0:
+            segs = [(b, 2 * j - 1, 1), (b, 2 * j, 1)]
+        else:
+            segs = [(b, 2 * j - 1, 2)]
+        units.append(segs)
+
+    with ExitStack() as ctx:
+        ctx.enter_context(tc.manual_schedule())
+        keep = ctx.enter_context(tc.tile_pool(name="keep", bufs=1))
+        work = ctx.enter_context(tc.tile_pool(name="work", bufs=2))
+        psum = ctx.enter_context(tc.psum_pool(name="psum", bufs=1))
+
+        w_raw = work.tile([P, T, RANK], BF16, name="w_raw", bufs=1)
+        nc.sync.dma_start(out=w_raw[:], in_=U_c_in.rearrange("(p j) r -> p j r", j=T))
+        taps_b = keep.tile([P, 3, 16], BF16, name="taps_b")
+        for i, u in enumerate((U_kh, U_kd, U_kw)):
+            nc.scalar.dma_start(out=taps_b[:, i, 0:3 * T].rearrange("p (k t) -> p k t", t=T), in_=u.rearrange("k (p t) -> p k t", t=T))
+        xs = keep.tile([P, T], F32, name="xs")
+        nc.scalar.dma_start(out=xs[:], in_=x_scale.rearrange("o (p t) a b c -> p (o t a b c)", t=T))
+        bias_b = keep.tile([P, 2], BF16, name="bias_b")
+        nc.scalar.dma_start(out=bias_b[:], in_=bias.rearrange("(p m) -> p m", m=2))
+        wo_raw = work.tile([P, T, COUT], BF16, name="wo_raw", bufs=1)
+        nc.scalar.dma_start(out=wo_raw[:], in_=U_c_out.rearrange("(p j) o -> p j o", j=T))
+
+        xb = {}
+
+        def load(s):
+            if s >= STEPS:
+                return
+            b, j = divmod(s, STEPS_B)
+            xb_t = work.tile([P, T, COLS], U8, name="xb_t", bufs=6)
+            src = x_bytes[b].rearrange("(p t) h w d -> p t (h w d)", t=T)
+            nc.sync.dma_start(out=xb_t[:], in_=src[:, :, j * COLS:(j + 1) * COLS])
+            xb[s] = xb_t
+
+        for s in range(5):
+            load(s)
+
+        v1 = [keep.tile([P, VOL], F32, name="v1_%d" % t) for t in range(T)]
+        v2 = [keep.tile([P, 4 + RING * SIDE * PITCH + 4], F32, name="v2_%d" % t) for t in range(T)]
+        for t in range(T):
+            nc.vector.memset(v2[t][:, 0:4], 0.0)
+            pads = v2[t][:, 4:4 + RING * SIDE * PITCH].rearrange("p (r c) -> p r c", c=PITCH)
+            nc.vector.memset(pads[:, :, SIDE:PITCH], 0.0)
+
+        taps = keep.tile([P, 3, 3, T], F32, name="taps")
+        nc.vector.tensor_copy(out=taps[:].rearrange("p a k t -> p a (k t)"), in_=taps_b[:, :, 0:3 * T])
+        bias_f = keep.tile([P, 2], F32, name="bias_f")
+        nc.vector.tensor_copy(out=bias_f[:], in_=bias_b[:])
+        mag = keep.tile([P, 2, 3, T], F32, name="mag")
+        nc.vector.scalar_tensor_tensor(out=mag[:], in0=taps[:, 0:2, :, :], scalar=-1.0, in1=taps[:, 0:2, :, :], op0=MULT, op1=MAX)
+        eps = keep.tile([P, 2, T], F32, name="eps")
+        nc.vector.tensor_tensor(out=eps[:], in0=mag[:, :, 0, :], in1=mag[:, :, 2, :], op=MAX)
+        nc.vector.tensor_scalar(out=eps[:], in0=eps[:], scalar1=2.0 ** -24, scalar2=2.0 ** -100, op0=MULT, op1=MAX)
+        small = keep.tile([P, 2, T], F32, name="small")
+        nc.vector.tensor_tensor(out=small[:], in0=mag[:, :, 1, :], in1=eps[:], op=LT)
+        mid = keep.tile([P, 2, T], F32, name="mid")
+        nc.vector.tensor_tensor(out=eps[:], in0=eps[:], in1=taps[:, 0:2, 1, :], op=SUB)
+        nc.vector.tensor_tensor(out=eps[:], in0=eps[:], in1=small[:], op=MULT)
+        nc.vector.tensor_tensor(out=mid[:], in0=taps[:, 0:2, 1, :], in1=eps[:], op=ADD)
+        inv = keep.tile([P, 2, T], F32, name="inv")
+        nc.vector.reciprocal(out=inv[:], in_=mid[:])
+        ratio = keep.tile([P, 2, 2, T], F32, name="ratio")
+        nc.vector.tensor_tensor(out=ratio[:, :, 0, :], in0=taps[:, 0:2, 0, :], in1=inv[:], op=MULT)
+        nc.vector.tensor_tensor(out=ratio[:, :, 1, :], in0=taps[:, 0:2, 2, :], in1=inv[:], op=MULT)
+        prod = keep.tile([P, T], F32, name="prod")
+        nc.vector.tensor_tensor(out=prod[:], in0=mid[:, 0, :], in1=mid[:, 1, :], op=MULT)
+        wsc = keep.tile([P, 3, T], F32, name="wsc")
+        for k in range(3):
+            nc.vector.tensor_tensor(out=wsc[:, k, :], in0=taps[:, 2, k, :], in1=prod[:], op=MULT)
+
+        ident = keep.tile([P, P], F32, name="ident")
+        make_identity(nc, ident[:])
+        diag = keep.tile([P, T, 2, P], F32, name="diag")
+        for t in range(T):
+            for k in range(2):
+                nc.gpsimd.tensor_scalar(out=diag[:, t, k, :], in0=ident[:], scalar1=ratio[:, 1, k, t:t + 1], scalar2=0.0, op0=MULT, op1=ADD)
+
+        wi_c = keep.tile([P, RANK], U32, name="wi_c", align_bytes=64)
+        wi_s = keep.tile([P, RANK], U8, name="wi_s", align_bytes=64)
+        wo_c = keep.tile([P, COUT], U32, name="wo_c", align_bytes=64)
+        wo_s = keep.tile([P, COUT], U8, name="wo_s", align_bytes=64)
+        w_grp = work.tile([P, RANK * T], BF16, name="w_grp", bufs=1, align_bytes=64)
+        wo_grp = work.tile([P, COUT * T], BF16, name="wo_grp", bufs=1, align_bytes=64)
+
+        def w_in_group():
+            nc.vector.tensor_copy(out=w_grp[:].rearrange("p (t m j) -> p t m j", t=T, j=T), in_=w_raw[:].rearrange("p j (m t) -> p t m j", t=T))
+
+        def w_in_quant():
+            nc.vector.quantize_mx(out=wi_c[:].bitcast(FP8X4), scales=wi_s[:], in_=w_grp[:])
+
+        def w_out_group():
+            nc.scalar.copy(out=wo_grp[:].rearrange("p (m q j) -> p m q j", m=2, j=T), in_=wo_raw[:].rearrange("p j (q m) -> p m q j", m=2))
+
+        def w_out_quant():
+            nc.vector.quantize_mx(out=wo_c[:].bitcast(FP8X4), scales=wo_s[:], in_=wo_grp[:])
+
+        xw, xi, xq, y0, zt, y3, pd, yi, yq, mo = {}, {}, {}, {}, {}, {}, {}, {}, {}, {}
+
+        def interleave(copy, dst, src, c0, c1):
+            copy(
+                out=dst[:, c0 * T:c1 * T].rearrange("p (c i t) -> p c t i", t=T, i=4),
+                in_=src[:, :, c0:c1].rearrange("p t (c i) -> p c t i", i=4),
+            )
+
+        def widen(s):
+            if s >= STEPS:
+                return
+            xw_t = work.tile([P, T, COLS], BF16, name="xw_t", bufs=2)
+            for t in range(T):
+                nc.scalar.activation(out=xw_t[:, t, :], in_=xb[s][:, t, :].bitcast(FP8), func=COPY, scale=xs[:, t:t + 1])
+            xw[s] = xw_t
+
+        def x_group_s(s):
+            if s >= STEPS:
+                return
+            xi_t = work.tile([P, COLS * T], BF16, name="xi_t", bufs=2, align_bytes=64)
+            xi[s] = xi_t
+            if CX_S > 0:
+                interleave(nc.scalar.copy, xi_t, xw[s], 0, CX_S)
+
+        def x_group_v(s):
+            if s >= STEPS:
+                return
+            if CX_S < COLS:
+                interleave(nc.vector.tensor_copy, xi[s], xw[s], CX_S, COLS)
+
+        def x_quant(s):
+            if s >= STEPS:
+                return
+            xq_c = work.tile([P, COLS], U32, name="xq_c", bufs=2, align_bytes=64)
+            xq_s = work.tile([P, COLS], U8, name="xq_s", bufs=2, align_bytes=64)
+            nc.vector.quantize_mx(out=xq_c[:].bitcast(FP8X4), scales=xq_s[:], in_=xi[s][:])
+            xq[s] = (xq_c, xq_s)
+
+        def mm1(s):
+            if s >= STEPS:
+                return
+            c, sc = xq[s]
+            for t in range(T):
+                y0_t = psum.tile([P, COLS], F32, name="y0_t", bufs=5)
+                nc.tensor.matmul_mx(
+                    out=y0_t[:],
+                    lhsT=wi_c[:, t * P:(t + 1) * P].bitcast(FP8X4), lhsT_scale=wi_s[:, t * P:(t + 1) * P],
+                    rhs=c[:].bitcast(FP8X4), rhs_scale=sc[:],
+                    start=True, stop=True,
+                )
+                y0[s, t] = y0_t
+
+        def v1_rows(t, s):
+            j = s % STEPS_B
+            return v1[t][:, j * COLS:(j + 1) * COLS]
+
+        def evac(s):
+            if s >= STEPS:
+                return
+            for t in range(T):
+                nc.scalar.activation(out=v1_rows(t, s), in_=y0[s, t][:], func=COPY, scale=wsc[:, 1, t:t + 1])
+
+        def w_filter(s):
+            if s >= STEPS:
+                return
+            n = PLANE - SIDE
+            for pair in (0, 2):
+                for k in (0, 2):
+                    for t in (pair, pair + 1):
+                        src = y0[s, t][:].rearrange("p (h c) -> p h c", c=PLANE)
+                        dst = v1_rows(t, s).rearrange("p (h c) -> p h c", c=PLANE)
+                        i, o = (slice(0, n), slice(SIDE, PLANE)) if k == 0 else (slice(SIDE, PLANE), slice(0, n))
+                        nc.vector.scalar_tensor_tensor(
+                            out=dst[:, :, o], in0=src[:, :, i], scalar=wsc[:, k, t:t + 1], in1=dst[:, :, o], op0=MULT, op1=ADD)
+
+        def v2_view(t, h, rows, shift, r0=0, r1=None):
+            r1 = rows * SIDE if r1 is None else r1
+            a = 4 + shift + ((h % RING) * SIDE + r0) * PITCH
+            b = a + (r1 - r0 - 1) * PITCH + SIDE
+            n = r1 - r0
+            if shift > 0:
+                return v2[t][:, a:a + n * PITCH].rearrange("p (r c) -> p r c", c=PITCH)[:, :, 0:SIDE]
+            return v2[t][:, a:a + n * PITCH].rearrange("p (r c) -> p r c", c=PITCH)[:, :, 0:SIDE]
+
+        def rows16(ap):
+            return ap.rearrange("p (r c) -> p r c", c=SIDE)
+
+        def h_scale(s):
+            if s >= STEPS:
+                return
+            j = s % STEPS_B
+            for t in range(T):
+                z_t = work.tile([P, COLS], F32, name="z_t", bufs=6)
+                c0 = PLANE if j == 0 else 0
+                nc.scalar.activation(out=z_t[:, c0:], in_=v1_rows(t, s)[:, c0:], func=COPY, scale=ratio[:, 0, 1, t:t + 1])
+                zt[s, t] = z_t
+
+        def h_first(s):
+            if s >= STEPS:
+                return
+            j = s % STEPS_B
+            h0 = 1 if j == 0 else 2 * j
+            n = 2 * j + 2 - h0
+            for t in range(T):
+                nc.vector.scalar_tensor_tensor(
+                    out=v2_view(t, h0, n, 0),
+                    in0=rows16(v1[t][:, (h0 - 1) * PLANE:(h0 - 1 + n) * PLANE]), scalar=ratio[:, 0, 0, t:t + 1],
+                    in1=rows16(v1[t][:, h0 * PLANE:(h0 + n) * PLANE]), op0=MULT, op1=ADD)
+
+        def h_second(s):
+            if s < 0 or s >= STEPS:
+                return
+            j = s % STEPS_B
+            for t in range(T):
+                if j == 0:
+                    nc.gpsimd.tensor_tensor(out=v2_view(t, 0, 1, 0), in0=rows16(v1[t][:, 0:PLANE]), in1=rows16(zt[s, t][:, PLANE:]), op=ADD)
+                else:
+                    c = 0
+                    for (b, h, rows) in units[s]:
+                        nc.gpsimd.tensor_tensor(
+                            out=v2_view(t, h, rows, 0), in0=v2_view(t, h, rows, 0),
+                            in1=rows16(zt[s, t][:, c:c + rows * PLANE]), op=ADD)
+                        c += rows * PLANE
+
+        def split(u):
+            total = sum(rows for (b, h, rows) in units[u]) * SIDE
+            pe = PE_ROWS * total // 32
+            pieces = []
+            r = 0
+            for (b, h, rows) in units[u]:
+                n = rows * SIDE
+                last = r + n == total
+                pieces.append((h, n - pe if last else n, r))
+                r += n
+            return total * SIDE, (total - pe) * SIDE, pe, pieces
+
+        def d_filter(u):
+            if u < 0 or u > STEPS:
+                return
+            n, nv, pe, pieces = split(u)
+            y3_t = work.tile([P, T, COLS], BF16, name="y3_t", bufs=2)
+            tmp = {}
+
+            def first(t):
+                tmp_t = work.tile([P, COLS], F32, name="tmp_t", bufs=3)
+                for (h, r, at) in pieces:
+                    nc.vector.scalar_tensor_tensor(
+                        out=rows16(tmp_t[:, at * SIDE:(at + r) * SIDE]), in0=v2_view(t, h, 1, -1, 0, r), scalar=ratio[:, 1, 0, t:t + 1],
+                        in1=v2_view(t, h, 1, 0, 0, r), op0=MULT, op1=ADD)
+                tmp[t] = tmp_t
+
+            def second(t):
+                for (h, r, at) in pieces:
+                    nc.vector.scalar_tensor_tensor(
+                        out=rows16(y3_t[:, t, at * SIDE:(at + r) * SIDE]), in0=v2_view(t, h, 1, 1, 0, r), scalar=ratio[:, 1, 1, t:t + 1],
+                        in1=rows16(tmp[t][:, at * SIDE:(at + r) * SIDE]), op0=MULT, op1=ADD)
+
+            first(0)
+            for t in range(1, T):
+                first(t)
+                second(t - 1)
+            second(T - 1)
+            y3[u] = y3_t
+            if pe:
+                h, r, at = pieces[-1]
+                pd_t = psum.tile([P, T, 128], F32, name="pd_t", bufs=1)
+                for t in range(T):
+                    for i, (shift, w) in enumerate(((-1, diag[:, t, 0, :]), (0, ident[:]), (1, diag[:, t, 1, :]))):
+                        nc.tensor.matmul(
+                            out=pd_t[:, t, 0:pe * SIDE], lhsT=w, rhs=v2_view(t, h, 1, shift, r, r + pe),
+                            start=(i == 0), stop=(i == 2))
+                pd[u] = pd_t
+
+        def y_group(u):
+            if u < 0 or u > STEPS:
+                return
+            n, nv, pe, pieces = split(u)
+            yi_t = work.tile([P, COLS * T], BF16, name="yi_t", bufs=2, align_bytes=64)
+            if pe:
+                nc.scalar.copy(out=yi_t[:, nv * T:n * T].rearrange("p (n t) -> p n t", t=T), in_=pd[u][:, :, 0:pe * SIDE].rearrange("p t n -> p n t"))
+            interleave(nc.scalar.copy, yi_t, y3[u], 0, nv)
+            yi[u] = yi_t
+
+        def y_quant(u):
+            if u < 0 or u > STEPS:
+                return
+            n = split(u)[0]
+            yq_c = work.tile([P, COLS], U32, name="yq_c", bufs=2, align_bytes=64)
+            yq_s = work.tile([P, COLS], U8, name="yq_s", bufs=2, align_bytes=64)
+            nc.vector.quantize_mx(out=yq_c[:, 0:n].bitcast(FP8X4), scales=yq_s[:, 0:n], in_=yi[u][:, 0:n * T])
+            yq[u] = (yq_c, yq_s)
+
+        def mm2(u):
+            if u < 0 or u > STEPS:
+                return
+            n = split(u)[0]
+            c, sc = yq[u]
+            for m in range(2):
+                mo_t = psum.tile([P, COLS], F32, name="mo_t", bufs=2)
+                nc.tensor.matmul_mx(
+                    out=mo_t[:, 0:n],
+                    lhsT=wo_c[:, m * P:(m + 1) * P].bitcast(FP8X4), lhsT_scale=wo_s[:, m * P:(m + 1) * P],
+                    rhs=c[:, 0:n].bitcast(FP8X4), rhs_scale=sc[:, 0:n],
+                    start=True, stop=True,
+                )
+                mo[u, m] = mo_t
+
+        def finish(u):
+            if u < 0 or u > STEPS:
+                return
+            n = split(u)[0]
+            for m in range(2):
+                o_t = work.tile([P, COLS], F32, name="o_t", bufs=4)
+                nc.scalar.activation(out=o_t[:, 0:n], in_=mo[u, m][:, 0:n], func=IDENT, bias=bias_f[:, m:m + 1])
+                c = 0
+                for (b, h, rows) in units[u]:
+                    dst = out[b].rearrange("(p m) h w d -> m p (h w d)", m=2)[m]
+                    nc.sync.dma_start(out=dst[:, h * PLANE:(h + rows) * PLANE], in_=o_t[:, c:c + rows * PLANE])
+                    c += rows * PLANE
+
+        widen(0)
+        w_in_group()
+        w_in_quant()
+        x_group_s(0)
+        x_group_v(0)
+        x_quant(0)
+        mm1(0)
+        widen(1)
+        evac(0)
+        x_group_s(1)
+        x_group_v(1)
+        w_out_group()
+        w_out_quant()
+
+        for s in range(STEPS + 3):
+            load(s + 5)
+            y_group(s - 2)
+            w_filter(s)
+            h_second(s - 1)
+            x_quant(s + 1)
+            mm1(s + 1)
+            y_quant(s - 2)
+            mm2(s - 2)
+            widen(s + 2)
+            h_scale(s)
+            d_filter(s - 1)
+            evac(s + 1)
+            x_group_s(s + 2)
+            x_group_v(s + 2)
+            h_first(s)
+            finish(s - 2)

@@ -28,7 +28,11 @@ STEPS_B = VOL // COLS
 PITCH = 20
 RING = 8
 PE_ROWS = 6
-CX_S = 384
+CX_S = 448
+ORDER = (3, 0, 1, 2)
+WIDEN_V = {0: (2, 3), 1: (1, 2, 3), 2: (2, 3)}
+CX_HEAD = {0: 256, 1: 0, 2: 128}
+FIN_V = (0,)
 
 FLOPS = 2 * BATCH * VOL * RANK * (CIN + COUT)
 
@@ -36,19 +40,18 @@ FLOPS = 2 * BATCH * VOL * RANK * (CIN + COUT)
 def tile_lowrankconv3d_t_kernel(tc, x_bytes, x_scale, U_kh, U_kw, U_kd, U_c_in, U_c_out, bias, out):
     nc = tc.nc
     units = []
-    for s in range(STEPS + 1):
+    for s in range(STEPS - 1):
         b, j = divmod(s, STEPS_B)
-        segs = []
         if j == 0:
-            if s > 0:
-                segs.append((b - 1, SIDE - 1, 1))
-            if s < STEPS:
-                segs.append((b, 0, 1))
+            segs = [(b - 1, SIDE - 1, 1)] if b > 0 else []
+            segs.append((b, 0, 1))
         elif (2 * j) % RING == 0:
             segs = [(b, 2 * j - 1, 1), (b, 2 * j, 1)]
         else:
             segs = [(b, 2 * j - 1, 2)]
         units.append(segs)
+    for h in range(SIDE - 3, SIDE):
+        units.append([(BATCH - 1, h, 1)])
 
     with ExitStack() as ctx:
         ctx.enter_context(tc.manual_schedule())
@@ -57,12 +60,11 @@ def tile_lowrankconv3d_t_kernel(tc, x_bytes, x_scale, U_kh, U_kw, U_kd, U_c_in, 
         psum = ctx.enter_context(tc.psum_pool(name="psum", bufs=1))
 
         w_raw = work.tile([P, T, RANK], BF16, name="w_raw", bufs=1)
-        nc.sync.dma_start(out=w_raw[:], in_=U_c_in.rearrange("(p j) r -> p j r", j=T))
+        xs = keep.tile([P, T], F32, name="xs")
+        nc.scalar.dma_start(out=xs[:], in_=x_scale.rearrange("o (p t) a b c -> p (o t a b c)", t=T))
         taps_b = keep.tile([P, 3, 16], BF16, name="taps_b")
         for i, u in enumerate((U_kh, U_kd, U_kw)):
             nc.scalar.dma_start(out=taps_b[:, i, 0:3 * T].rearrange("p (k t) -> p k t", t=T), in_=u.rearrange("k (p t) -> p k t", t=T))
-        xs = keep.tile([P, T], F32, name="xs")
-        nc.scalar.dma_start(out=xs[:], in_=x_scale.rearrange("o (p t) a b c -> p (o t a b c)", t=T))
         bias_b = keep.tile([P, 2], BF16, name="bias_b")
         nc.scalar.dma_start(out=bias_b[:], in_=bias.rearrange("(p m) -> p m", m=2))
         wo_raw = work.tile([P, T, COUT], BF16, name="wo_raw", bufs=1)
@@ -79,7 +81,9 @@ def tile_lowrankconv3d_t_kernel(tc, x_bytes, x_scale, U_kh, U_kw, U_kd, U_c_in, 
             nc.sync.dma_start(out=xb_t[:], in_=src[:, :, j * COLS:(j + 1) * COLS])
             xb[s] = xb_t
 
-        for s in range(5):
+        load(0)
+        nc.sync.dma_start(out=w_raw[:], in_=U_c_in.rearrange("(p j) r -> p j r", j=T))
+        for s in range(1, 5):
             load(s)
 
         v1 = [keep.tile([P, VOL], F32, name="v1_%d" % t) for t in range(T)]
@@ -90,37 +94,46 @@ def tile_lowrankconv3d_t_kernel(tc, x_bytes, x_scale, U_kh, U_kw, U_kd, U_c_in, 
             nc.vector.memset(pads[:, :, SIDE:PITCH], 0.0)
 
         taps = keep.tile([P, 3, 3, T], F32, name="taps")
-        nc.vector.tensor_copy(out=taps[:].rearrange("p a k t -> p a (k t)"), in_=taps_b[:, :, 0:3 * T])
         bias_f = keep.tile([P, 2], F32, name="bias_f")
-        nc.vector.tensor_copy(out=bias_f[:], in_=bias_b[:])
         mag = keep.tile([P, 2, 3, T], F32, name="mag")
-        nc.vector.scalar_tensor_tensor(out=mag[:], in0=taps[:, 0:2, :, :], scalar=-1.0, in1=taps[:, 0:2, :, :], op0=MULT, op1=MAX)
         eps = keep.tile([P, 2, T], F32, name="eps")
-        nc.vector.tensor_tensor(out=eps[:], in0=mag[:, :, 0, :], in1=mag[:, :, 2, :], op=MAX)
-        nc.vector.tensor_scalar(out=eps[:], in0=eps[:], scalar1=2.0 ** -24, scalar2=2.0 ** -100, op0=MULT, op1=MAX)
+        gap = keep.tile([P, 2, T], F32, name="gap")
         small = keep.tile([P, 2, T], F32, name="small")
-        nc.vector.tensor_tensor(out=small[:], in0=mag[:, :, 1, :], in1=eps[:], op=LT)
         mid = keep.tile([P, 2, T], F32, name="mid")
-        nc.vector.tensor_tensor(out=eps[:], in0=eps[:], in1=taps[:, 0:2, 1, :], op=SUB)
-        nc.vector.tensor_tensor(out=eps[:], in0=eps[:], in1=small[:], op=MULT)
-        nc.vector.tensor_tensor(out=mid[:], in0=taps[:, 0:2, 1, :], in1=eps[:], op=ADD)
         inv = keep.tile([P, 2, T], F32, name="inv")
-        nc.vector.reciprocal(out=inv[:], in_=mid[:])
         ratio = keep.tile([P, 2, 2, T], F32, name="ratio")
-        nc.vector.tensor_tensor(out=ratio[:, :, 0, :], in0=taps[:, 0:2, 0, :], in1=inv[:], op=MULT)
-        nc.vector.tensor_tensor(out=ratio[:, :, 1, :], in0=taps[:, 0:2, 2, :], in1=inv[:], op=MULT)
         prod = keep.tile([P, T], F32, name="prod")
-        nc.vector.tensor_tensor(out=prod[:], in0=mid[:, 0, :], in1=mid[:, 1, :], op=MULT)
         wsc = keep.tile([P, 3, T], F32, name="wsc")
-        for k in range(3):
-            nc.vector.tensor_tensor(out=wsc[:, k, :], in0=taps[:, 2, k, :], in1=prod[:], op=MULT)
+        tt = nc.vector.tensor_tensor
+        tap_steps = [
+            lambda: nc.vector.tensor_copy(out=taps[:].rearrange("p a k t -> p a (k t)"), in_=taps_b[:, :, 0:3 * T]),
+            lambda: nc.vector.scalar_tensor_tensor(out=mag[:], in0=taps[:, 0:2, :, :], scalar=-1.0, in1=taps[:, 0:2, :, :], op0=MULT, op1=MAX),
+            lambda: tt(out=eps[:], in0=mag[:, :, 0, :], in1=mag[:, :, 2, :], op=MAX),
+            lambda: nc.vector.tensor_scalar(out=eps[:], in0=eps[:], scalar1=2.0 ** -24, scalar2=2.0 ** -100, op0=MULT, op1=MAX),
+            lambda: (tt(out=small[:], in0=mag[:, :, 1, :], in1=eps[:], op=LT), tt(out=gap[:], in0=eps[:], in1=taps[:, 0:2, 1, :], op=SUB)),
+            lambda: tt(out=gap[:], in0=gap[:], in1=small[:], op=MULT),
+            lambda: tt(out=mid[:], in0=taps[:, 0:2, 1, :], in1=gap[:], op=ADD),
+            lambda: (tt(out=prod[:], in0=mid[:, 0, :], in1=mid[:, 1, :], op=MULT), nc.vector.reciprocal(out=inv[:], in_=mid[:])),
+            lambda: [tt(out=wsc[:, k, :], in0=taps[:, 2, k, :], in1=prod[:], op=MULT) for k in (1, 0, 2)],
+            lambda: [tt(out=ratio[:, :, i, :], in0=taps[:, 0:2, 2 * i, :], in1=inv[:], op=MULT) for i in range(2)],
+            lambda: nc.vector.tensor_copy(out=bias_f[:], in_=bias_b[:]),
+        ]
+
+        def tap_step(n=1):
+            for i in range(n):
+                if tap_steps:
+                    step = tap_steps[0]
+                    tap_steps.remove(step)
+                    step()
 
         ident = keep.tile([P, P], F32, name="ident")
         make_identity(nc, ident[:])
         diag = keep.tile([P, T, 2, P], F32, name="diag")
-        for t in range(T):
-            for k in range(2):
-                nc.gpsimd.tensor_scalar(out=diag[:, t, k, :], in0=ident[:], scalar1=ratio[:, 1, k, t:t + 1], scalar2=0.0, op0=MULT, op1=ADD)
+
+        def make_diag():
+            for t in range(T):
+                for k in range(2):
+                    nc.gpsimd.tensor_scalar(out=diag[:, t, k, :], in0=ident[:], scalar1=ratio[:, 1, k, t:t + 1], scalar2=0.0, op0=MULT, op1=ADD)
 
         wi_c = keep.tile([P, RANK], U32, name="wi_c", align_bytes=64)
         wi_s = keep.tile([P, RANK], U8, name="wi_s", align_bytes=64)
@@ -129,14 +142,15 @@ def tile_lowrankconv3d_t_kernel(tc, x_bytes, x_scale, U_kh, U_kw, U_kd, U_c_in, 
         w_grp = work.tile([P, RANK * T], BF16, name="w_grp", bufs=1, align_bytes=64)
         wo_grp = work.tile([P, COUT * T], BF16, name="wo_grp", bufs=1, align_bytes=64)
 
-        def w_in_group():
-            nc.vector.tensor_copy(out=w_grp[:].rearrange("p (t m j) -> p t m j", t=T, j=T), in_=w_raw[:].rearrange("p j (m t) -> p t m j", t=T))
+        def w_in_group(copy, t0, t1):
+            copy(out=w_grp[:].rearrange("p (t m j) -> p t m j", t=T, j=T)[:, t0:t1], in_=w_raw[:].rearrange("p j (m t) -> p t m j", t=T)[:, t0:t1])
 
-        def w_in_quant():
-            nc.vector.quantize_mx(out=wi_c[:].bitcast(FP8X4), scales=wi_s[:], in_=w_grp[:])
+        def w_in_quant(t0, t1):
+            n = slice(t0 * P, t1 * P)
+            nc.vector.quantize_mx(out=wi_c[:, n].bitcast(FP8X4), scales=wi_s[:, n], in_=w_grp[:, t0 * P * T:t1 * P * T])
 
         def w_out_group():
-            nc.scalar.copy(out=wo_grp[:].rearrange("p (m q j) -> p m q j", m=2, j=T), in_=wo_raw[:].rearrange("p j (q m) -> p m q j", m=2))
+            nc.gpsimd.tensor_scalar(out=wo_grp[:].rearrange("p (m q j) -> p m q j", m=2, j=T), in0=wo_raw[:].rearrange("p j (q m) -> p m q j", m=2), scalar1=1.0, scalar2=0.0, op0=MULT, op1=ADD)
 
         def w_out_quant():
             nc.vector.quantize_mx(out=wo_c[:].bitcast(FP8X4), scales=wo_s[:], in_=wo_grp[:])
@@ -153,23 +167,30 @@ def tile_lowrankconv3d_t_kernel(tc, x_bytes, x_scale, U_kh, U_kw, U_kd, U_c_in, 
             if s >= STEPS:
                 return
             xw_t = work.tile([P, T, COLS], BF16, name="xw_t", bufs=2)
-            for t in range(T):
-                nc.scalar.activation(out=xw_t[:, t, :], in_=xb[s][:, t, :].bitcast(FP8), func=COPY, scale=xs[:, t:t + 1])
             xw[s] = xw_t
+            for t in range(T):
+                if t not in WIDEN_V.get(s, ()):
+                    nc.scalar.activation(out=xw_t[:, t, :], in_=xb[s][:, t, :].bitcast(FP8), func=COPY, scale=xs[:, t:t + 1])
+
+        def widen_v(s):
+            for t in WIDEN_V.get(s, ()):
+                nc.vector.tensor_scalar(out=xw[s][:, t, :], in0=xb[s][:, t, :].bitcast(FP8), scalar1=xs[:, t:t + 1], scalar2=None, op0=MULT)
 
         def x_group_s(s):
             if s >= STEPS:
                 return
             xi_t = work.tile([P, COLS * T], BF16, name="xi_t", bufs=2, align_bytes=64)
             xi[s] = xi_t
-            if CX_S > 0:
-                interleave(nc.scalar.copy, xi_t, xw[s], 0, CX_S)
+            cx = CX_HEAD.get(s, CX_S)
+            if cx > 0:
+                interleave(nc.scalar.copy, xi_t, xw[s], 0, cx)
 
         def x_group_v(s):
             if s >= STEPS:
                 return
-            if CX_S < COLS:
-                interleave(nc.vector.tensor_copy, xi[s], xw[s], CX_S, COLS)
+            cx = CX_HEAD.get(s, CX_S)
+            if cx < COLS:
+                interleave(nc.vector.tensor_copy, xi[s], xw[s], cx, COLS)
 
         def x_quant(s):
             if s >= STEPS:
@@ -232,7 +253,7 @@ def tile_lowrankconv3d_t_kernel(tc, x_bytes, x_scale, U_kh, U_kw, U_kd, U_c_in, 
             if s >= STEPS:
                 return
             j = s % STEPS_B
-            for t in range(T):
+            for t in ORDER if s < STEPS - 1 else ():
                 z_t = work.tile([P, COLS], F32, name="z_t", bufs=6)
                 c0 = PLANE if j == 0 else 0
                 nc.scalar.activation(out=z_t[:, c0:], in_=v1_rows(t, s)[:, c0:], func=COPY, scale=ratio[:, 0, 1, t:t + 1])
@@ -254,7 +275,7 @@ def tile_lowrankconv3d_t_kernel(tc, x_bytes, x_scale, U_kh, U_kw, U_kd, U_c_in, 
             if s < 0 or s >= STEPS:
                 return
             j = s % STEPS_B
-            for t in range(T):
+            for t in ORDER:
                 if j == 0:
                     nc.gpsimd.tensor_tensor(out=v2_view(t, 0, 1, 0), in0=rows16(v1[t][:, 0:PLANE]), in1=rows16(zt[s, t][:, PLANE:]), op=ADD)
                 else:
@@ -264,6 +285,12 @@ def tile_lowrankconv3d_t_kernel(tc, x_bytes, x_scale, U_kh, U_kw, U_kd, U_c_in, 
                             out=v2_view(t, h, rows, 0), in0=v2_view(t, h, rows, 0),
                             in1=rows16(zt[s, t][:, c:c + rows * PLANE]), op=ADD)
                         c += rows * PLANE
+
+        def h_second_v(h):
+            for t in range(T):
+                nc.vector.scalar_tensor_tensor(
+                    out=v2_view(t, h, 1, 0), in0=rows16(v1[t][:, (h + 1) * PLANE:(h + 2) * PLANE]),
+                    scalar=ratio[:, 0, 1, t:t + 1], in1=v2_view(t, h, 1, 0), op0=MULT, op1=ADD)
 
         def split(u):
             total = sum(rows for (b, h, rows) in units[u]) * SIDE
@@ -278,7 +305,7 @@ def tile_lowrankconv3d_t_kernel(tc, x_bytes, x_scale, U_kh, U_kw, U_kd, U_c_in, 
             return total * SIDE, (total - pe) * SIDE, pe, pieces
 
         def d_filter(u):
-            if u < 0 or u > STEPS:
+            if u < 0:
                 return
             n, nv, pe, pieces = split(u)
             y3_t = work.tile([P, T, COLS], BF16, name="y3_t", bufs=2)
@@ -298,34 +325,47 @@ def tile_lowrankconv3d_t_kernel(tc, x_bytes, x_scale, U_kh, U_kw, U_kd, U_c_in, 
                         out=rows16(y3_t[:, t, at * SIDE:(at + r) * SIDE]), in0=v2_view(t, h, 1, 1, 0, r), scalar=ratio[:, 1, 1, t:t + 1],
                         in1=rows16(tmp[t][:, at * SIDE:(at + r) * SIDE]), op0=MULT, op1=ADD)
 
-            first(0)
-            for t in range(1, T):
-                first(t)
-                second(t - 1)
-            second(T - 1)
+            order = ORDER
+            first(order[0])
+            for i in range(1, T):
+                first(order[i])
+                second(order[i - 1])
+            second(order[T - 1])
             y3[u] = y3_t
+
+        def d_filter_pe(u):
+            if u < 0:
+                return
+            n, nv, pe, pieces = split(u)
             if pe:
                 h, r, at = pieces[-1]
                 pd_t = psum.tile([P, T, 128], F32, name="pd_t", bufs=1)
-                for t in range(T):
+                for t in ORDER:
                     for i, (shift, w) in enumerate(((-1, diag[:, t, 0, :]), (0, ident[:]), (1, diag[:, t, 1, :]))):
                         nc.tensor.matmul(
                             out=pd_t[:, t, 0:pe * SIDE], lhsT=w, rhs=v2_view(t, h, 1, shift, r, r + pe),
                             start=(i == 0), stop=(i == 2))
                 pd[u] = pd_t
 
-        def y_group(u):
-            if u < 0 or u > STEPS:
+        def y_group(u, s_cols=0):
+            if u < 0:
                 return
             n, nv, pe, pieces = split(u)
             yi_t = work.tile([P, COLS * T], BF16, name="yi_t", bufs=2, align_bytes=64)
-            if pe:
-                nc.scalar.copy(out=yi_t[:, nv * T:n * T].rearrange("p (n t) -> p n t", t=T), in_=pd[u][:, :, 0:pe * SIDE].rearrange("p t n -> p n t"))
-            interleave(nc.scalar.copy, yi_t, y3[u], 0, nv)
             yi[u] = yi_t
+            interleave(nc.scalar.copy, yi_t, y3[u], 0, s_cols or nv)
+            if s_cols:
+                interleave(nc.vector.tensor_copy, yi_t, y3[u], s_cols, nv)
+
+        def y_group_pe(u):
+            if u < 0:
+                return
+            n, nv, pe, pieces = split(u)
+            if pe:
+                nc.scalar.copy(out=yi[u][:, nv * T:n * T].rearrange("p (n t) -> p n t", t=T), in_=pd[u][:, :, 0:pe * SIDE].rearrange("p t n -> p n t"))
 
         def y_quant(u):
-            if u < 0 or u > STEPS:
+            if u < 0:
                 return
             n = split(u)[0]
             yq_c = work.tile([P, COLS], U32, name="yq_c", bufs=2, align_bytes=64)
@@ -334,7 +374,7 @@ def tile_lowrankconv3d_t_kernel(tc, x_bytes, x_scale, U_kh, U_kw, U_kd, U_c_in, 
             yq[u] = (yq_c, yq_s)
 
         def mm2(u):
-            if u < 0 or u > STEPS:
+            if u < 0:
                 return
             n = split(u)[0]
             c, sc = yq[u]
@@ -348,47 +388,98 @@ def tile_lowrankconv3d_t_kernel(tc, x_bytes, x_scale, U_kh, U_kw, U_kd, U_c_in, 
                 )
                 mo[u, m] = mo_t
 
-        def finish(u):
-            if u < 0 or u > STEPS:
+        def finish(u, on_v, on_s):
+            if u < 0:
                 return
             n = split(u)[0]
-            for m in range(2):
+            for m in on_v + on_s:
                 o_t = work.tile([P, COLS], F32, name="o_t", bufs=4)
-                nc.scalar.activation(out=o_t[:, 0:n], in_=mo[u, m][:, 0:n], func=IDENT, bias=bias_f[:, m:m + 1])
+                if m in on_v:
+                    nc.vector.tensor_scalar(out=o_t[:, 0:n], in0=mo[u, m][:, 0:n], scalar1=bias_f[:, m:m + 1], scalar2=None, op0=ADD)
+                else:
+                    nc.scalar.activation(out=o_t[:, 0:n], in_=mo[u, m][:, 0:n], func=IDENT, bias=bias_f[:, m:m + 1])
                 c = 0
                 for (b, h, rows) in units[u]:
                     dst = out[b].rearrange("(p m) h w d -> m p (h w d)", m=2)[m]
                     nc.sync.dma_start(out=dst[:, h * PLANE:(h + rows) * PLANE], in_=o_t[:, c:c + rows * PLANE])
                     c += rows * PLANE
 
+        tap_step(3)
         widen(0)
-        w_in_group()
-        w_in_quant()
+        widen_v(0)
+        tap_step()
         x_group_s(0)
         x_group_v(0)
+        tap_step()
+        w_in_group(nc.vector.tensor_copy, 0, 2)
+        w_in_group(nc.scalar.copy, 2, 4)
+        tap_step()
         x_quant(0)
+        tap_step()
+        w_in_quant(0, 2)
+        tap_step()
+        w_in_quant(2, 4)
         mm1(0)
+        tap_step()
         widen(1)
         evac(0)
+        widen_v(1)
+        tap_step(2)
+        make_diag()
+        w_out_group()
         x_group_s(1)
         x_group_v(1)
-        w_out_group()
-        w_out_quant()
 
-        for s in range(STEPS + 3):
+        for s in range(STEPS):
             load(s + 5)
             y_group(s - 2)
+            y_group_pe(s - 2)
             w_filter(s)
             h_second(s - 1)
+            finish(s - 3, FIN_V, tuple(m for m in range(2) if m not in FIN_V))
             x_quant(s + 1)
             mm1(s + 1)
+            if s == 1:
+                w_out_quant()
             y_quant(s - 2)
             mm2(s - 2)
             widen(s + 2)
+            widen_v(s + 2)
             h_scale(s)
+            d_filter_pe(s - 1)
             d_filter(s - 1)
             evac(s + 1)
             x_group_s(s + 2)
             x_group_v(s + 2)
             h_first(s)
-            finish(s - 2)
+
+        u = STEPS - 2
+        finish(u - 1, (), (0, 1))
+        y_group(u)
+        y_group_pe(u)
+        d_filter(u + 3)
+        d_filter_pe(u + 3)
+        h_second_v(SIDE - 3)
+        y_quant(u)
+        mm2(u)
+        d_filter(u + 1)
+        y_group(u + 3)
+        y_group_pe(u + 3)
+        d_filter_pe(u + 1)
+        h_second_v(SIDE - 2)
+        d_filter_pe(u + 2)
+        y_quant(u + 3)
+        finish(u, (), (0, 1))
+        mm2(u + 3)
+        y_group(u + 1)
+        y_group_pe(u + 1)
+        finish(u + 3, (), (0, 1))
+        d_filter(u + 2)
+        y_quant(u + 1)
+        mm2(u + 1)
+        y_group(u + 2, 96)
+        y_group_pe(u + 2)
+        y_quant(u + 2)
+        finish(u + 1, (0,), (1,))
+        mm2(u + 2)
+        finish(u + 2, (0,), (1,))

@@ -26,13 +26,16 @@ COLS = 512
 STEPS = BATCH * VOL // COLS
 STEPS_B = VOL // COLS
 PITCH = 20
-RING = 8
+RING = 12
+NO_PE = (STEPS - 1, STEPS, STEPS + 1)
 PE_ROWS = 6
 CX_S = 448
-ORDER = (3, 0, 1, 2)
+G_GROUPS = ((1, 4),)
+V_ADD = (0,)
+H_ORDER = (0, 1, 2, 3)
 WIDEN_V = {0: (2, 3), 1: (1, 2, 3), 2: (2, 3)}
 CX_HEAD = {0: 256, 1: 0, 2: 128}
-FIN_V = (0,)
+FIN_V = ()
 
 FLOPS = 2 * BATCH * VOL * RANK * (CIN + COUT)
 
@@ -86,11 +89,11 @@ def tile_lowrankconv3d_t_kernel(tc, x_bytes, x_scale, U_kh, U_kw, U_kd, U_c_in, 
         for s in range(1, 5):
             load(s)
 
-        v1 = [keep.tile([P, VOL], F32, name="v1_%d" % t) for t in range(T)]
-        v2 = [keep.tile([P, 4 + RING * SIDE * PITCH + 4], F32, name="v2_%d" % t) for t in range(T)]
+        v1 = keep.tile([P, T, VOL], F32, name="v1")
+        v2 = keep.tile([P, T, 4 + RING * SIDE * PITCH + 4], F32, name="v2")
         for t in range(T):
-            nc.vector.memset(v2[t][:, 0:4], 0.0)
-            pads = v2[t][:, 4:4 + RING * SIDE * PITCH].rearrange("p (r c) -> p r c", c=PITCH)
+            nc.vector.memset(v2[:, t, 0:4], 0.0)
+            pads = v2[:, t, 4:4 + RING * SIDE * PITCH].rearrange("p (r c) -> p r c", c=PITCH)
             nc.vector.memset(pads[:, :, SIDE:PITCH], 0.0)
 
         taps = keep.tile([P, 3, 3, T], F32, name="taps")
@@ -216,7 +219,7 @@ def tile_lowrankconv3d_t_kernel(tc, x_bytes, x_scale, U_kh, U_kw, U_kd, U_c_in, 
 
         def v1_rows(t, s):
             j = s % STEPS_B
-            return v1[t][:, j * COLS:(j + 1) * COLS]
+            return v1[:, t, j * COLS:(j + 1) * COLS]
 
         def evac(s):
             if s >= STEPS:
@@ -240,11 +243,14 @@ def tile_lowrankconv3d_t_kernel(tc, x_bytes, x_scale, U_kh, U_kw, U_kd, U_c_in, 
         def v2_view(t, h, rows, shift, r0=0, r1=None):
             r1 = rows * SIDE if r1 is None else r1
             a = 4 + shift + ((h % RING) * SIDE + r0) * PITCH
-            b = a + (r1 - r0 - 1) * PITCH + SIDE
-            n = r1 - r0
-            if shift > 0:
-                return v2[t][:, a:a + n * PITCH].rearrange("p (r c) -> p r c", c=PITCH)[:, :, 0:SIDE]
-            return v2[t][:, a:a + n * PITCH].rearrange("p (r c) -> p r c", c=PITCH)[:, :, 0:SIDE]
+            return v2[:, t, a:a + (r1 - r0) * PITCH].rearrange("p (r c) -> p r c", c=PITCH)[:, :, 0:SIDE]
+
+        def v2_rows(ts, h, rows):
+            a = 4 + (h % RING) * SIDE * PITCH
+            return v2[:, ts[0]:ts[1], a:a + rows * SIDE * PITCH].rearrange("p t (r c) -> p t r c", c=PITCH)[:, :, :, 0:SIDE]
+
+        def rows16t(ap):
+            return ap.rearrange("p t (r c) -> p t r c", c=SIDE)
 
         def rows16(ap):
             return ap.rearrange("p (r c) -> p r c", c=SIDE)
@@ -253,11 +259,14 @@ def tile_lowrankconv3d_t_kernel(tc, x_bytes, x_scale, U_kh, U_kw, U_kd, U_c_in, 
             if s >= STEPS:
                 return
             j = s % STEPS_B
-            for t in ORDER if s < STEPS - 1 else ():
-                z_t = work.tile([P, COLS], F32, name="z_t", bufs=6)
-                c0 = PLANE if j == 0 else 0
-                nc.scalar.activation(out=z_t[:, c0:], in_=v1_rows(t, s)[:, c0:], func=COPY, scale=ratio[:, 0, 1, t:t + 1])
-                zt[s, t] = z_t
+            if s == STEPS - 1:
+                return
+            z_t = work.tile([P, T, COLS], F32, name="z_t", bufs=2)
+            c0 = PLANE if j == 0 else 0
+            for t in range(T):
+                if t not in V_ADD:
+                    nc.scalar.activation(out=z_t[:, t, c0:], in_=v1_rows(t, s)[:, c0:], func=COPY, scale=ratio[:, 0, 1, t:t + 1])
+            zt[s] = z_t
 
         def h_first(s):
             if s >= STEPS:
@@ -265,36 +274,49 @@ def tile_lowrankconv3d_t_kernel(tc, x_bytes, x_scale, U_kh, U_kw, U_kd, U_c_in, 
             j = s % STEPS_B
             h0 = 1 if j == 0 else 2 * j
             n = 2 * j + 2 - h0
-            for t in range(T):
+            for t in H_ORDER:
                 nc.vector.scalar_tensor_tensor(
                     out=v2_view(t, h0, n, 0),
-                    in0=rows16(v1[t][:, (h0 - 1) * PLANE:(h0 - 1 + n) * PLANE]), scalar=ratio[:, 0, 0, t:t + 1],
-                    in1=rows16(v1[t][:, h0 * PLANE:(h0 + n) * PLANE]), op0=MULT, op1=ADD)
+                    in0=rows16(v1[:, t, (h0 - 1) * PLANE:(h0 - 1 + n) * PLANE]), scalar=ratio[:, 0, 0, t:t + 1],
+                    in1=rows16(v1[:, t, h0 * PLANE:(h0 + n) * PLANE]), op0=MULT, op1=ADD)
 
         def h_second(s):
             if s < 0 or s >= STEPS:
                 return
             j = s % STEPS_B
-            for t in ORDER:
-                if j == 0:
-                    nc.gpsimd.tensor_tensor(out=v2_view(t, 0, 1, 0), in0=rows16(v1[t][:, 0:PLANE]), in1=rows16(zt[s, t][:, PLANE:]), op=ADD)
-                else:
-                    c = 0
-                    for (b, h, rows) in units[s]:
-                        nc.gpsimd.tensor_tensor(
-                            out=v2_view(t, h, rows, 0), in0=v2_view(t, h, rows, 0),
-                            in1=rows16(zt[s, t][:, c:c + rows * PLANE]), op=ADD)
-                        c += rows * PLANE
+            for ts in G_GROUPS:
+                a, b = ts
+                c = PLANE if j == 0 else 0
+                for (b_, h, rows) in units[s]:
+                    if j == 0 and h != 0:
+                        continue
+                    old = v1[:, a:b, 0:PLANE] if j == 0 else None
+                    nc.gpsimd.tensor_tensor(
+                        out=v2_rows(ts, h, rows), in0=rows16t(old) if j == 0 else v2_rows(ts, h, rows),
+                        in1=rows16t(zt[s][:, a:b, c:c + rows * PLANE]), op=ADD)
+                    c += rows * PLANE
+
+        def h_second_some(s):
+            if s < 0:
+                return
+            for t in V_ADD:
+                for (b_, h, rows) in units[s]:
+                    if h == SIDE - 1:
+                        continue
+                    in1 = rows16(v1[:, t, 0:PLANE]) if h == 0 else v2_view(t, h, rows, 0)
+                    nc.vector.scalar_tensor_tensor(
+                        out=v2_view(t, h, rows, 0), in0=rows16(v1[:, t, (h + 1) * PLANE:(h + 1 + rows) * PLANE]),
+                        scalar=ratio[:, 0, 1, t:t + 1], in1=in1, op0=MULT, op1=ADD)
 
         def h_second_v(h):
             for t in range(T):
                 nc.vector.scalar_tensor_tensor(
-                    out=v2_view(t, h, 1, 0), in0=rows16(v1[t][:, (h + 1) * PLANE:(h + 2) * PLANE]),
+                    out=v2_view(t, h, 1, 0), in0=rows16(v1[:, t, (h + 1) * PLANE:(h + 2) * PLANE]),
                     scalar=ratio[:, 0, 1, t:t + 1], in1=v2_view(t, h, 1, 0), op0=MULT, op1=ADD)
 
         def split(u):
             total = sum(rows for (b, h, rows) in units[u]) * SIDE
-            pe = PE_ROWS * total // 32
+            pe = 0 if u in NO_PE else PE_ROWS * total // 32
             pieces = []
             r = 0
             for (b, h, rows) in units[u]:
@@ -325,7 +347,7 @@ def tile_lowrankconv3d_t_kernel(tc, x_bytes, x_scale, U_kh, U_kw, U_kd, U_c_in, 
                         out=rows16(y3_t[:, t, at * SIDE:(at + r) * SIDE]), in0=v2_view(t, h, 1, 1, 0, r), scalar=ratio[:, 1, 1, t:t + 1],
                         in1=rows16(tmp[t][:, at * SIDE:(at + r) * SIDE]), op0=MULT, op1=ADD)
 
-            order = ORDER
+            order = tuple(range(T))
             first(order[0])
             for i in range(1, T):
                 first(order[i])
@@ -340,7 +362,7 @@ def tile_lowrankconv3d_t_kernel(tc, x_bytes, x_scale, U_kh, U_kw, U_kd, U_c_in, 
             if pe:
                 h, r, at = pieces[-1]
                 pd_t = psum.tile([P, T, 128], F32, name="pd_t", bufs=1)
-                for t in ORDER:
+                for t in range(T):
                     for i, (shift, w) in enumerate(((-1, diag[:, t, 0, :]), (0, ident[:]), (1, diag[:, t, 1, :]))):
                         nc.tensor.matmul(
                             out=pd_t[:, t, 0:pe * SIDE], lhsT=w, rhs=v2_view(t, h, 1, shift, r, r + pe),
@@ -437,6 +459,7 @@ def tile_lowrankconv3d_t_kernel(tc, x_bytes, x_scale, U_kh, U_kw, U_kd, U_c_in, 
             w_filter(s)
             h_second(s - 1)
             finish(s - 3, FIN_V, tuple(m for m in range(2) if m not in FIN_V))
+            h_second_some(s - 1)
             x_quant(s + 1)
             mm1(s + 1)
             if s == 1:

@@ -28,14 +28,11 @@ STEPS_B = VOL // COLS
 PITCH = 20
 RING = 12
 NO_PE = (STEPS - 1, STEPS, STEPS + 1)
-PE_ROWS = 6
-CX_S = 448
-G_GROUPS = ((1, 4),)
-V_ADD = (0,)
-H_ORDER = (0, 1, 2, 3)
+PE_ROWS = 7
+CX_S = 384
+V_ROWS = 4
 WIDEN_V = {0: (2, 3), 1: (1, 2, 3), 2: (2, 3)}
 CX_HEAD = {0: 256, 1: 0, 2: 128}
-FIN_V = ()
 
 FLOPS = 2 * BATCH * VOL * RANK * (CIN + COUT)
 
@@ -245,9 +242,9 @@ def tile_lowrankconv3d_t_kernel(tc, x_bytes, x_scale, U_kh, U_kw, U_kd, U_c_in, 
             a = 4 + shift + ((h % RING) * SIDE + r0) * PITCH
             return v2[:, t, a:a + (r1 - r0) * PITCH].rearrange("p (r c) -> p r c", c=PITCH)[:, :, 0:SIDE]
 
-        def v2_rows(ts, h, rows):
+        def v2_all(h, n):
             a = 4 + (h % RING) * SIDE * PITCH
-            return v2[:, ts[0]:ts[1], a:a + rows * SIDE * PITCH].rearrange("p t (r c) -> p t r c", c=PITCH)[:, :, :, 0:SIDE]
+            return v2[:, :, a:a + n * PITCH].rearrange("p t (r c) -> p t r c", c=PITCH)[:, :, :, 0:SIDE]
 
         def rows16t(ap):
             return ap.rearrange("p t (r c) -> p t r c", c=SIDE)
@@ -263,9 +260,9 @@ def tile_lowrankconv3d_t_kernel(tc, x_bytes, x_scale, U_kh, U_kw, U_kd, U_c_in, 
                 return
             z_t = work.tile([P, T, COLS], F32, name="z_t", bufs=2)
             c0 = PLANE if j == 0 else 0
+            c1 = COLS - V_ROWS * SIDE
             for t in range(T):
-                if t not in V_ADD:
-                    nc.scalar.activation(out=z_t[:, t, c0:], in_=v1_rows(t, s)[:, c0:], func=COPY, scale=ratio[:, 0, 1, t:t + 1])
+                nc.scalar.activation(out=z_t[:, t, c0:c1], in_=v1_rows(t, s)[:, c0:c1], func=COPY, scale=ratio[:, 0, 1, t:t + 1])
             zt[s] = z_t
 
         def h_first(s):
@@ -274,7 +271,7 @@ def tile_lowrankconv3d_t_kernel(tc, x_bytes, x_scale, U_kh, U_kw, U_kd, U_c_in, 
             j = s % STEPS_B
             h0 = 1 if j == 0 else 2 * j
             n = 2 * j + 2 - h0
-            for t in H_ORDER:
+            for t in range(T):
                 nc.vector.scalar_tensor_tensor(
                     out=v2_view(t, h0, n, 0),
                     in0=rows16(v1[:, t, (h0 - 1) * PLANE:(h0 - 1 + n) * PLANE]), scalar=ratio[:, 0, 0, t:t + 1],
@@ -283,30 +280,27 @@ def tile_lowrankconv3d_t_kernel(tc, x_bytes, x_scale, U_kh, U_kw, U_kd, U_c_in, 
         def h_second(s):
             if s < 0 or s >= STEPS:
                 return
-            j = s % STEPS_B
-            for ts in G_GROUPS:
-                a, b = ts
-                c = PLANE if j == 0 else 0
-                for (b_, h, rows) in units[s]:
-                    if j == 0 and h != 0:
-                        continue
-                    old = v1[:, a:b, 0:PLANE] if j == 0 else None
-                    nc.gpsimd.tensor_tensor(
-                        out=v2_rows(ts, h, rows), in0=rows16t(old) if j == 0 else v2_rows(ts, h, rows),
-                        in1=rows16t(zt[s][:, a:b, c:c + rows * PLANE]), op=ADD)
-                    c += rows * PLANE
+            c = PLANE if s % STEPS_B == 0 else 0
+            for (h, n, first) in h_pieces(s):
+                old = rows16t(v1[:, :, 0:n * SIDE]) if first else v2_all(h, n)
+                nc.gpsimd.tensor_tensor(out=v2_all(h, n), in0=old, in1=rows16t(zt[s][:, :, c:c + n * SIDE]), op=ADD)
+                c += n * SIDE
+
+        def h_pieces(s):
+            segs = [(h, rows * SIDE, h == 0) for (b, h, rows) in units[s] if h < SIDE - 1]
+            h, n, first = segs[-1]
+            return segs[:-1] + [(h, n - V_ROWS, first)]
 
         def h_second_some(s):
-            if s < 0:
+            if s < 0 or V_ROWS == 0:
                 return
-            for t in V_ADD:
-                for (b_, h, rows) in units[s]:
-                    if h == SIDE - 1:
-                        continue
-                    in1 = rows16(v1[:, t, 0:PLANE]) if h == 0 else v2_view(t, h, rows, 0)
-                    nc.vector.scalar_tensor_tensor(
-                        out=v2_view(t, h, rows, 0), in0=rows16(v1[:, t, (h + 1) * PLANE:(h + 1 + rows) * PLANE]),
-                        scalar=ratio[:, 0, 1, t:t + 1], in1=in1, op0=MULT, op1=ADD)
+            h, n, first = h_pieces(s)[-1]
+            for t in range(T):
+                a = h * PLANE + n * SIDE
+                new = v2_view(t, h, 1, 0, n, n + V_ROWS)
+                nc.vector.scalar_tensor_tensor(
+                    out=new, in0=rows16(v1[:, t, a + PLANE:a + PLANE + V_ROWS * SIDE]), scalar=ratio[:, 0, 1, t:t + 1],
+                    in1=rows16(v1[:, t, a:a + V_ROWS * SIDE]) if first else new, op0=MULT, op1=ADD)
 
         def h_second_v(h):
             for t in range(T):
@@ -426,10 +420,9 @@ def tile_lowrankconv3d_t_kernel(tc, x_bytes, x_scale, U_kh, U_kw, U_kd, U_c_in, 
                     nc.sync.dma_start(out=dst[:, h * PLANE:(h + rows) * PLANE], in_=o_t[:, c:c + rows * PLANE])
                     c += rows * PLANE
 
-        tap_step(3)
         widen(0)
         widen_v(0)
-        tap_step()
+        tap_step(4)
         x_group_s(0)
         x_group_v(0)
         tap_step()
@@ -454,27 +447,27 @@ def tile_lowrankconv3d_t_kernel(tc, x_bytes, x_scale, U_kh, U_kw, U_kd, U_c_in, 
 
         for s in range(STEPS):
             load(s + 5)
+            widen(s + 2)
             y_group(s - 2)
             y_group_pe(s - 2)
             w_filter(s)
             h_second(s - 1)
-            finish(s - 3, FIN_V, tuple(m for m in range(2) if m not in FIN_V))
-            h_second_some(s - 1)
             x_quant(s + 1)
-            mm1(s + 1)
+            finish(s - 3, (), (0, 1))
+            h_second_some(s - 1)
             if s == 1:
                 w_out_quant()
+            mm1(s + 1)
             y_quant(s - 2)
             mm2(s - 2)
-            widen(s + 2)
             widen_v(s + 2)
             h_scale(s)
             d_filter_pe(s - 1)
             d_filter(s - 1)
             evac(s + 1)
+            h_first(s)
             x_group_s(s + 2)
             x_group_v(s + 2)
-            h_first(s)
 
         u = STEPS - 2
         finish(u - 1, (), (0, 1))

from contextlib import ExitStack

import concourse.mybir as mybir
from concourse.masks import make_identity

F32 = mybir.dt.float32
BF16 = mybir.dt.bfloat16
U32 = mybir.dt.uint32
U8 = mybir.dt.uint8
FP8 = mybir.dt.float8_e4m3fn
FP8X4 = mybir.dt.float8_e4m3fn_x4
ADD = mybir.AluOpType.add
SUB = mybir.AluOpType.subtract
MULT = mybir.AluOpType.mult
MAX = mybir.AluOpType.max
LT = mybir.AluOpType.is_lt
COPY = mybir.ActivationFunctionType.Copy
IDENT = mybir.ActivationFunctionType.Identity

P = 128
T = 4
BATCH, CIN, RANK, COUT, SIDE = 2, 512, 512, 256, 16
PLANE = SIDE * SIDE
VOL = SIDE * PLANE
COLS = 512
STEPS = BATCH * VOL // COLS
STEPS_B = VOL // COLS
PITCH = 20
RING = 12
NO_PE = (STEPS - 1, STEPS, STEPS + 1)
PE_ROWS = 7
CX_S = 384
V_ROWS = 4
WIDEN_V = {0: (2, 3), 1: (1, 2, 3), 2: (2, 3)}
CX_HEAD = {0: 256, 1: 0, 2: 128}

FLOPS = 2 * BATCH * VOL * RANK * (CIN + COUT)


def tile_lowrankconv3d_t_kernel(tc, x_bytes, x_scale, U_kh, U_kw, U_kd, U_c_in, U_c_out, bias, out):
    nc = tc.nc
    units = []
    for s in range(STEPS - 1):
        b, j = divmod(s, STEPS_B)
        if j == 0:
            segs = [(b - 1, SIDE - 1, 1)] if b > 0 else []
            segs.append((b, 0, 1))
        elif (2 * j) % RING == 0:
            segs = [(b, 2 * j - 1, 1), (b, 2 * j, 1)]
        else:
            segs = [(b, 2 * j - 1, 2)]
        units.append(segs)
    for h in range(SIDE - 3, SIDE):
        units.append([(BATCH - 1, h, 1)])

    with ExitStack() as ctx:
        ctx.enter_context(tc.manual_schedule())
        keep = ctx.enter_context(tc.tile_pool(name="keep", bufs=1))
        work = ctx.enter_context(tc.tile_pool(name="work", bufs=2))
        psum = ctx.enter_context(tc.psum_pool(name="psum", bufs=1))

        w_raw = work.tile([P, T, RANK], BF16, name="w_raw", bufs=1)
        xs = keep.tile([P, T], F32, name="xs")
        nc.scalar.dma_start(out=xs[:], in_=x_scale.rearrange("o (p t) a b c -> p (o t a b c)", t=T))
        taps_b = keep.tile([P, 3, 16], BF16, name="taps_b")
        for i, u in enumerate((U_kh, U_kd, U_kw)):
            nc.scalar.dma_start(out=taps_b[:, i, 0:3 * T].rearrange("p (k t) -> p k t", t=T), in_=u.rearrange("k (p t) -> p k t", t=T))
        bias_b = keep.tile([P, 2], BF16, name="bias_b")
        nc.scalar.dma_start(out=bias_b[:], in_=bias.rearrange("(p m) -> p m", m=2))
        wo_raw = work.tile([P, T, COUT], BF16, name="wo_raw", bufs=1)
        nc.scalar.dma_start(out=wo_raw[:], in_=U_c_out.rearrange("(p j) o -> p j o", j=T))

        xb = {}

        def load(s):
            if s >= STEPS:
                return
            b, j = divmod(s, STEPS_B)
            xb_t = work.tile([P, T, COLS], U8, name="xb_t", bufs=6)
            src = x_bytes[b].rearrange("(p t) h w d -> p t (h w d)", t=T)
            nc.sync.dma_start(out=xb_t[:], in_=src[:, :, j * COLS:(j + 1) * COLS])
            xb[s] = xb_t

        load(0)
        nc.sync.dma_start(out=w_raw[:], in_=U_c_in.rearrange("(p j) r -> p j r", j=T))
        for s in range(1, 5):
            load(s)

        v1 = keep.tile([P, T, VOL], F32, name="v1")
        v2 = keep.tile([P, T, 4 + RING * SIDE * PITCH + 4], F32, name="v2")
        for t in range(T):
            nc.vector.memset(v2[:, t, 0:4], 0.0)
            pads = v2[:, t, 4:4 + RING * SIDE * PITCH].rearrange("p (r c) -> p r c", c=PITCH)
            nc.vector.memset(pads[:, :, SIDE:PITCH], 0.0)

        taps = keep.tile([P, 3, 3, T], F32, name="taps")
        bias_f = keep.tile([P, 2], F32, name="bias_f")
        mag = keep.tile([P, 2, 3, T], F32, name="mag")
        eps = keep.tile([P, 2, T], F32, name="eps")
        gap = keep.tile([P, 2, T], F32, name="gap")
        small = keep.tile([P, 2, T], F32, name="small")
        mid = keep.tile([P, 2, T], F32, name="mid")
        inv = keep.tile([P, 2, T], F32, name="inv")
        ratio = keep.tile([P, 2, 2, T], F32, name="ratio")
        prod = keep.tile([P, T], F32, name="prod")
        wsc = keep.tile([P, 3, T], F32, name="wsc")
        tt = nc.vector.tensor_tensor
        tap_steps = [
            lambda: nc.vector.tensor_copy(out=taps[:].rearrange("p a k t -> p a (k t)"), in_=taps_b[:, :, 0:3 * T]),
            lambda: nc.vector.scalar_tensor_tensor(out=mag[:], in0=taps[:, 0:2, :, :], scalar=-1.0, in1=taps[:, 0:2, :, :], op0=MULT, op1=MAX),
            lambda: tt(out=eps[:], in0=mag[:, :, 0, :], in1=mag[:, :, 2, :], op=MAX),
            lambda: nc.vector.tensor_scalar(out=eps[:], in0=eps[:], scalar1=2.0 ** -24, scalar2=2.0 ** -100, op0=MULT, op1=MAX),
            lambda: (tt(out=small[:], in0=mag[:, :, 1, :], in1=eps[:], op=LT), tt(out=gap[:], in0=eps[:], in1=taps[:, 0:2, 1, :], op=SUB)),
            lambda: tt(out=gap[:], in0=gap[:], in1=small[:], op=MULT),
            lambda: tt(out=mid[:], in0=taps[:, 0:2, 1, :], in1=gap[:], op=ADD),
            lambda: (tt(out=prod[:], in0=mid[:, 0, :], in1=mid[:, 1, :], op=MULT), nc.vector.reciprocal(out=inv[:], in_=mid[:])),
            lambda: [tt(out=wsc[:, k, :], in0=taps[:, 2, k, :], in1=prod[:], op=MULT) for k in (1, 0, 2)],
            lambda: [tt(out=ratio[:, :, i, :], in0=taps[:, 0:2, 2 * i, :], in1=inv[:], op=MULT) for i in range(2)],
            lambda: nc.vector.tensor_copy(out=bias_f[:], in_=bias_b[:]),
        ]

        def tap_step(n=1):
            for i in range(n):
                if tap_steps:
                    step = tap_steps[0]
                    tap_steps.remove(step)
                    step()

        ident = keep.tile([P, P], F32, name="ident")
        make_identity(nc, ident[:])
        diag = keep.tile([P, T, 2, P], F32, name="diag")

        def make_diag():
            for t in range(T):
                for k in range(2):
                    nc.gpsimd.tensor_scalar(out=diag[:, t, k, :], in0=ident[:], scalar1=ratio[:, 1, k, t:t + 1], scalar2=0.0, op0=MULT, op1=ADD)

        wi_c = keep.tile([P, RANK], U32, name="wi_c", align_bytes=64)
        wi_s = keep.tile([P, RANK], U8, name="wi_s", align_bytes=64)
        wo_c = keep.tile([P, COUT], U32, name="wo_c", align_bytes=64)
        wo_s = keep.tile([P, COUT], U8, name="wo_s", align_bytes=64)
        w_grp = work.tile([P, RANK * T], BF16, name="w_grp", bufs=1, align_bytes=64)
        wo_grp = work.tile([P, COUT * T], BF16, name="wo_grp", bufs=1, align_bytes=64)

        def w_in_group(copy, t0, t1):
            copy(out=w_grp[:].rearrange("p (t m j) -> p t m j", t=T, j=T)[:, t0:t1], in_=w_raw[:].rearrange("p j (m t) -> p t m j", t=T)[:, t0:t1])

        def w_in_quant(t0, t1):
            n = slice(t0 * P, t1 * P)
            nc.vector.quantize_mx(out=wi_c[:, n].bitcast(FP8X4), scales=wi_s[:, n], in_=w_grp[:, t0 * P * T:t1 * P * T])

        def w_out_group():
            nc.gpsimd.tensor_scalar(out=wo_grp[:].rearrange("p (m q j) -> p m q j", m=2, j=T), in0=wo_raw[:].rearrange("p j (q m) -> p m q j", m=2), scalar1=1.0, scalar2=0.0, op0=MULT, op1=ADD)

        def w_out_quant():
            nc.vector.quantize_mx(out=wo_c[:].bitcast(FP8X4), scales=wo_s[:], in_=wo_grp[:])

        xw, xi, xq, y0, zt, y3, pd, yi, yq, mo = {}, {}, {}, {}, {}, {}, {}, {}, {}, {}

        def interleave(copy, dst, src, c0, c1):
            copy(
                out=dst[:, c0 * T:c1 * T].rearrange("p (c i t) -> p c t i", t=T, i=4),
                in_=src[:, :, c0:c1].rearrange("p t (c i) -> p c t i", i=4),
            )

        def widen(s):
            if s >= STEPS:
                return
            xw_t = work.tile([P, T, COLS], BF16, name="xw_t", bufs=2)
            xw[s] = xw_t
            for t in range(T):
                if t not in WIDEN_V.get(s, ()):
                    nc.scalar.activation(out=xw_t[:, t, :], in_=xb[s][:, t, :].bitcast(FP8), func=COPY, scale=xs[:, t:t + 1])

        def widen_v(s):
            for t in WIDEN_V.get(s, ()):
                nc.vector.tensor_scalar(out=xw[s][:, t, :], in0=xb[s][:, t, :].bitcast(FP8), scalar1=xs[:, t:t + 1], scalar2=None, op0=MULT)

        def x_group_s(s):
            if s >= STEPS:
                return
            xi_t = work.tile([P, COLS * T], BF16, name="xi_t", bufs=2, align_bytes=64)
            xi[s] = xi_t
            cx = CX_HEAD.get(s, CX_S)
            if cx > 0:
                interleave(nc.scalar.copy, xi_t, xw[s], 0, cx)

        def x_group_v(s):
            if s >= STEPS:
                return
            cx = CX_HEAD.get(s, CX_S)
            if cx < COLS:
                interleave(nc.vector.tensor_copy, xi[s], xw[s], cx, COLS)

        def x_quant(s):
            if s >= STEPS:
                return
            xq_c = work.tile([P, COLS], U32, name="xq_c", bufs=2, align_bytes=64)
            xq_s = work.tile([P, COLS], U8, name="xq_s", bufs=2, align_bytes=64)
            nc.vector.quantize_mx(out=xq_c[:].bitcast(FP8X4), scales=xq_s[:], in_=xi[s][:])
            xq[s] = (xq_c, xq_s)

        def mm1(s):
            if s >= STEPS:
                return
            c, sc = xq[s]
            for t in range(T):
                y0_t = psum.tile([P, COLS], F32, name="y0_t", bufs=5)
                nc.tensor.matmul_mx(
                    out=y0_t[:],
                    lhsT=wi_c[:, t * P:(t + 1) * P].bitcast(FP8X4), lhsT_scale=wi_s[:, t * P:(t + 1) * P],
                    rhs=c[:].bitcast(FP8X4), rhs_scale=sc[:],
                    start=True, stop=True,
                )
                y0[s, t] = y0_t

        def v1_rows(t, s):
            j = s % STEPS_B
            return v1[:, t, j * COLS:(j + 1) * COLS]

        def evac(s):
            if s >= STEPS:
                return
            for t in range(T):
                nc.scalar.activation(out=v1_rows(t, s), in_=y0[s, t][:], func=COPY, scale=wsc[:, 1, t:t + 1])

        def w_filter(s):
            if s >= STEPS:
                return
            n = PLANE - SIDE
            for pair in (0, 2):
                for k in (0, 2):
                    for t in (pair, pair + 1):
                        src = y0[s, t][:].rearrange("p (h c) -> p h c", c=PLANE)
                        dst = v1_rows(t, s).rearrange("p (h c) -> p h c", c=PLANE)
                        i, o = (slice(0, n), slice(SIDE, PLANE)) if k == 0 else (slice(SIDE, PLANE), slice(0, n))
                        nc.vector.scalar_tensor_tensor(
                            out=dst[:, :, o], in0=src[:, :, i], scalar=wsc[:, k, t:t + 1], in1=dst[:, :, o], op0=MULT, op1=ADD)

        def v2_view(t, h, rows, shift, r0=0, r1=None):
            r1 = rows * SIDE if r1 is None else r1
            a = 4 + shift + ((h % RING) * SIDE + r0) * PITCH
            return v2[:, t, a:a + (r1 - r0) * PITCH].rearrange("p (r c) -> p r c", c=PITCH)[:, :, 0:SIDE]

        def v2_all(h, n):
            a = 4 + (h % RING) * SIDE * PITCH
            return v2[:, :, a:a + n * PITCH].rearrange("p t (r c) -> p t r c", c=PITCH)[:, :, :, 0:SIDE]

        def rows16t(ap):
            return ap.rearrange("p t (r c) -> p t r c", c=SIDE)

        def rows16(ap):
            return ap.rearrange("p (r c) -> p r c", c=SIDE)

        def h_scale(s):
            if s >= STEPS:
                return
            j = s % STEPS_B
            if s == STEPS - 1:
                return
            z_t = work.tile([P, T, COLS], F32, name="z_t", bufs=2)
            c0 = PLANE if j == 0 else 0
            c1 = COLS - V_ROWS * SIDE
            for t in range(T):
                nc.scalar.activation(out=z_t[:, t, c0:c1], in_=v1_rows(t, s)[:, c0:c1], func=COPY, scale=ratio[:, 0, 1, t:t + 1])
            zt[s] = z_t

        def h_first(s):
            if s >= STEPS:
                return
            j = s % STEPS_B
            h0 = 1 if j == 0 else 2 * j
            n = 2 * j + 2 - h0
            for t in range(T):
                nc.vector.scalar_tensor_tensor(
                    out=v2_view(t, h0, n, 0),
                    in0=rows16(v1[:, t, (h0 - 1) * PLANE:(h0 - 1 + n) * PLANE]), scalar=ratio[:, 0, 0, t:t + 1],
                    in1=rows16(v1[:, t, h0 * PLANE:(h0 + n) * PLANE]), op0=MULT, op1=ADD)

        def h_second(s):
            if s < 0 or s >= STEPS:
                return
            c = PLANE if s % STEPS_B == 0 else 0
            for (h, n, first) in h_pieces(s):
                old = rows16t(v1[:, :, 0:n * SIDE]) if first else v2_all(h, n)
                nc.gpsimd.tensor_tensor(out=v2_all(h, n), in0=old, in1=rows16t(zt[s][:, :, c:c + n * SIDE]), op=ADD)
                c += n * SIDE

        def h_pieces(s):
            segs = [(h, rows * SIDE, h == 0) for (b, h, rows) in units[s] if h < SIDE - 1]
            h, n, first = segs[-1]
            return segs[:-1] + [(h, n - V_ROWS, first)]

        def h_second_some(s):
            if s < 0 or V_ROWS == 0:
                return
            h, n, first = h_pieces(s)[-1]
            for t in range(T):
                a = h * PLANE + n * SIDE
                new = v2_view(t, h, 1, 0, n, n + V_ROWS)
                nc.vector.scalar_tensor_tensor(
                    out=new, in0=rows16(v1[:, t, a + PLANE:a + PLANE + V_ROWS * SIDE]), scalar=ratio[:, 0, 1, t:t + 1],
                    in1=rows16(v1[:, t, a:a + V_ROWS * SIDE]) if first else new, op0=MULT, op1=ADD)

        def h_second_v(h):
            for t in range(T):
                nc.vector.scalar_tensor_tensor(
                    out=v2_view(t, h, 1, 0), in0=rows16(v1[:, t, (h + 1) * PLANE:(h + 2) * PLANE]),
                    scalar=ratio[:, 0, 1, t:t + 1], in1=v2_view(t, h, 1, 0), op0=MULT, op1=ADD)

        def split(u):
            total = sum(rows for (b, h, rows) in units[u]) * SIDE
            pe = 0 if u in NO_PE else PE_ROWS * total // 32
            pieces = []
            r = 0
            for (b, h, rows) in units[u]:
                n = rows * SIDE
                last = r + n == total
                pieces.append((h, n - pe if last else n, r))
                r += n
            return total * SIDE, (total - pe) * SIDE, pe, pieces

        def d_filter(u):
            if u < 0:
                return
            n, nv, pe, pieces = split(u)
            y3_t = work.tile([P, T, COLS], BF16, name="y3_t", bufs=2)
            tmp = {}

            def first(t):
                tmp_t = work.tile([P, COLS], F32, name="tmp_t", bufs=3)
                for (h, r, at) in pieces:
                    nc.vector.scalar_tensor_tensor(
                        out=rows16(tmp_t[:, at * SIDE:(at + r) * SIDE]), in0=v2_view(t, h, 1, -1, 0, r), scalar=ratio[:, 1, 0, t:t + 1],
                        in1=v2_view(t, h, 1, 0, 0, r), op0=MULT, op1=ADD)
                tmp[t] = tmp_t

            def second(t):
                for (h, r, at) in pieces:
                    nc.vector.scalar_tensor_tensor(
                        out=rows16(y3_t[:, t, at * SIDE:(at + r) * SIDE]), in0=v2_view(t, h, 1, 1, 0, r), scalar=ratio[:, 1, 1, t:t + 1],
                        in1=rows16(tmp[t][:, at * SIDE:(at + r) * SIDE]), op0=MULT, op1=ADD)

            order = tuple(range(T))
            first(order[0])
            for i in range(1, T):
                first(order[i])
                second(order[i - 1])
            second(order[T - 1])
            y3[u] = y3_t

        def d_filter_pe(u):
            if u < 0:
                return
            n, nv, pe, pieces = split(u)
            if pe:
                h, r, at = pieces[-1]
                pd_t = psum.tile([P, T, 128], F32, name="pd_t", bufs=1)
                for t in range(T):
                    for i, (shift, w) in enumerate(((-1, diag[:, t, 0, :]), (0, ident[:]), (1, diag[:, t, 1, :]))):
                        nc.tensor.matmul(
                            out=pd_t[:, t, 0:pe * SIDE], lhsT=w, rhs=v2_view(t, h, 1, shift, r, r + pe),
                            start=(i == 0), stop=(i == 2))
                pd[u] = pd_t

        def y_group(u, s_cols=0):
            if u < 0:
                return
            n, nv, pe, pieces = split(u)
            yi_t = work.tile([P, COLS * T], BF16, name="yi_t", bufs=2, align_bytes=64)
            yi[u] = yi_t
            interleave(nc.scalar.copy, yi_t, y3[u], 0, s_cols or nv)
            if s_cols:
                interleave(nc.vector.tensor_copy, yi_t, y3[u], s_cols, nv)

        def y_group_pe(u):
            if u < 0:
                return
            n, nv, pe, pieces = split(u)
            if pe:
                nc.scalar.copy(out=yi[u][:, nv * T:n * T].rearrange("p (n t) -> p n t", t=T), in_=pd[u][:, :, 0:pe * SIDE].rearrange("p t n -> p n t"))

        def y_quant(u):
            if u < 0:
                return
            n = split(u)[0]
            yq_c = work.tile([P, COLS], U32, name="yq_c", bufs=2, align_bytes=64)
            yq_s = work.tile([P, COLS], U8, name="yq_s", bufs=2, align_bytes=64)
            nc.vector.quantize_mx(out=yq_c[:, 0:n].bitcast(FP8X4), scales=yq_s[:, 0:n], in_=yi[u][:, 0:n * T])
            yq[u] = (yq_c, yq_s)

        def mm2(u):
            if u < 0:
                return
            n = split(u)[0]
            c, sc = yq[u]
            for m in range(2):
                mo_t = psum.tile([P, COLS], F32, name="mo_t", bufs=2)
                nc.tensor.matmul_mx(
                    out=mo_t[:, 0:n],
                    lhsT=wo_c[:, m * P:(m + 1) * P].bitcast(FP8X4), lhsT_scale=wo_s[:, m * P:(m + 1) * P],
                    rhs=c[:, 0:n].bitcast(FP8X4), rhs_scale=sc[:, 0:n],
                    start=True, stop=True,
                )
                mo[u, m] = mo_t

        def finish(u, on_v, on_s):
            if u < 0:
                return
            n = split(u)[0]
            for m in on_v + on_s:
                o_t = work.tile([P, COLS], F32, name="o_t", bufs=4)
                if m in on_v:
                    nc.vector.tensor_scalar(out=o_t[:, 0:n], in0=mo[u, m][:, 0:n], scalar1=bias_f[:, m:m + 1], scalar2=None, op0=ADD)
                else:
                    nc.scalar.activation(out=o_t[:, 0:n], in_=mo[u, m][:, 0:n], func=IDENT, bias=bias_f[:, m:m + 1])
                c = 0
                for (b, h, rows) in units[u]:
                    dst = out[b].rearrange("(p m) h w d -> m p (h w d)", m=2)[m]
                    nc.sync.dma_start(out=dst[:, h * PLANE:(h + rows) * PLANE], in_=o_t[:, c:c + rows * PLANE])
                    c += rows * PLANE

        widen(0)
        widen_v(0)
        tap_step(4)
        x_group_s(0)
        x_group_v(0)
        tap_step()
        w_in_group(nc.vector.tensor_copy, 0, 2)
        w_in_group(nc.scalar.copy, 2, 4)
        tap_step()
        x_quant(0)
        tap_step()
        w_in_quant(0, 2)
        tap_step()
        w_in_quant(2, 4)
        mm1(0)
        tap_step()
        widen(1)
        evac(0)
        widen_v(1)
        tap_step(2)
        make_diag()
        w_out_group()
        x_group_s(1)
        x_group_v(1)

        for s in range(STEPS):
            load(s + 5)
            widen(s + 2)
            y_group(s - 2)
            y_group_pe(s - 2)
            w_filter(s)
            h_second(s - 1)
            x_quant(s + 1)
            finish(s - 3, (), (0, 1))
            h_second_some(s - 1)
            if s == 1:
                w_out_quant()
            mm1(s + 1)
            y_quant(s - 2)
            mm2(s - 2)
            widen_v(s + 2)
            h_scale(s)
            d_filter_pe(s - 1)
            d_filter(s - 1)
            evac(s + 1)
            h_first(s)
            x_group_s(s + 2)
            x_group_v(s + 2)

        u = STEPS - 2
        finish(u - 1, (), (0, 1))
        y_group(u)
        y_group_pe(u)
        d_filter(u + 3)
        d_filter_pe(u + 3)
        h_second_v(SIDE - 3)
        y_quant(u)
        mm2(u)
        d_filter(u + 1)
        y_group(u + 3)
        y_group_pe(u + 3)
        d_filter_pe(u + 1)
        h_second_v(SIDE - 2)
        d_filter_pe(u + 2)
        y_quant(u + 3)
        finish(u, (), (0, 1))
        mm2(u + 3)
        y_group(u + 1)
        y_group_pe(u + 1)
        finish(u + 3, (), (0, 1))
        d_filter(u + 2)
        y_quant(u + 1)
        mm2(u + 1)
        y_group(u + 2, 96)
        y_group_pe(u + 2)
        y_quant(u + 2)
        finish(u + 1, (0,), (1,))
        mm2(u + 2)
        finish(u + 2, (0,), (1,))
